import numpy as np
import ml_dtypes


def mxq(x, axis, fmt="e4m3"):
    dtype, down = {"e4m3": (ml_dtypes.float8_e4m3fn, 7), "e5m2": (ml_dtypes.float8_e5m2, 14)}[fmt]
    v = np.moveaxis(np.asarray(x, np.float32).astype(ml_dtypes.bfloat16).astype(np.float64), axis, -1)
    blocks = v.reshape(v.shape[:-1] + (-1, 32))
    amax = np.abs(blocks).max(-1, keepdims=True)
    byte = np.maximum(np.where(amax > 0, np.frexp(amax)[1] - 1 + 127, 0) - down, 1)
    scale = np.exp2(byte - 127.0)
    codes = (blocks / scale).astype(np.float32).astype(dtype).astype(np.float64)
    return np.moveaxis((codes * scale).reshape(v.shape), -1, axis)


WIDE = False


def mx_kscale(k):
    if not WIDE:
        return np.ones(k)
    levels = np.array([10, -10, 5, -5, 0])
    a = np.random.permutation(np.resize(levels, k // 512 * 4)).reshape(k // 512, 4)
    idx = np.arange(k)
    return np.exp2(a[idx // 512, idx % 128 // 32])


BF16 = ml_dtypes.bfloat16


def bf(x):
    return np.asarray(x, np.float32).astype(BF16)


def f64(x):
    return np.asarray(x).astype(np.float64)


NB, C, O, CZ, DD, HH, WW, MG = 1, 1024, 128, 128, 8, 16, 16, 4
STRIDES = (2, 2, 2)


def setup_inputs():
    s = mx_kscale(C)
    sd, sh, sw = STRIDES
    return {"x": bf(np.random.standard_normal((NB, C, DD, HH, WW)) * s[None, :, None, None, None]),
            "z": bf(np.random.standard_normal((NB, CZ, sd * DD + MG, sh * HH + MG, sw * WW + MG))),
            "W": bf(np.random.standard_normal((O, C)) / np.sqrt(C) / s[None, :]),
            "b": bf(np.random.standard_normal(O) * 0.5)}


def reference(x, z, W, b):
    sd, sh, sw = STRIDES
    u = np.repeat(np.repeat(np.repeat(f64(x), sd, axis=2), sh, axis=3), sw, axis=4)
    n, c, d, h, w = u.shape
    y = mxq(f64(W), 1, "e4m3") @ mxq(u.reshape(n, c, d * h * w), 1, "e4m3")
    y = y.reshape(n, -1, d, h, w) + f64(b)[None, :, None, None, None]
    zf = f64(z)
    off = [(zf.shape[i] - y.shape[i]) // 2 for i in range(2, 5)]
    zc = zf[:, :,
            off[0]:off[0] + y.shape[2],
            off[1]:off[1] + y.shape[3],
            off[2]:off[2] + y.shape[4]]
    return np.concatenate([y, zc], axis=1)

@@ -1,0 +1,159 @@
+import concourse.mybir as mybir
+from concourse.masks import make_identity
+
+F32 = mybir.dt.float32
+BF16 = mybir.dt.bfloat16
+U32 = mybir.dt.uint32
+U8 = mybir.dt.uint8
+FP8X4 = mybir.dt.float8_e4m3fn_x4
+IDENTITY = mybir.ActivationFunctionType.Identity
+
+P = 128
+PACK = 4
+K_PASS = P * PACK
+C_IN = 1024
+PASSES = C_IN // K_PASS
+C_OUT = 128
+D_IN, H_IN, W_IN = 8, 16, 16
+POS = D_IN * H_IN * W_IN
+SLICE = H_IN * W_IN
+CHUNK = 2 * SLICE
+N_CHUNKS = POS // CHUNK
+Z_SIDE = 36
+MARGIN = 2
+OUT_D, OUT_H, OUT_W = 16, 32, 32
+D_TILE = 4
+
+FLOPS = 2 * C_OUT * C_IN * OUT_D * OUT_H * OUT_W
+BYTES = (C_IN * POS * 2 + C_OUT * OUT_D * OUT_H * OUT_W * 2 + C_OUT * C_IN * 2 + C_OUT * 2
+         + 2 * C_OUT * OUT_D * OUT_H * OUT_W * 4)
+
+
+def tile_upconvcropcat_t_kernel(tc, x, z, W, b, out):
+    nc = tc.nc
+    x_rows = x[0].rearrange("c d h w -> c (d h w)")
+
+    with tc.tile_pool(name="consts", bufs=1) as consts, \
+            tc.tile_pool(name="xin", bufs=1) as xin, \
+            tc.tile_pool(name="zin", bufs=1) as zin, \
+            tc.tile_pool(name="grp", bufs=4) as grp, \
+            tc.tile_pool(name="mx", bufs=1) as mx, \
+            tc.tile_pool(name="ostage", bufs=6) as ostage, \
+            tc.psum_pool(name="psum", bufs=8) as psum:
+
+        w_sb = consts.tile([P, C_IN], BF16, name="w_sb")
+        nc.scalar.dma_start(out=w_sb[:], in_=W)
+        b_row = consts.tile([1, C_OUT], BF16, name="b_row")
+        nc.scalar.dma_start(out=b_row[:], in_=b.unsqueeze(0))
+
+        z_raw = [zin.tile([P, D_TILE, Z_SIDE, Z_SIDE], BF16, name="z_raw%d" % i) for i in range(4)]
+        x_raw = [xin.tile([P, PACK, POS], BF16, name="x_raw%d" % g) for g in range(PASSES)]
+
+        def load_z(i):
+            d0 = MARGIN + D_TILE * i
+            nc.sync.dma_start(out=z_raw[i][:], in_=z[0, :, d0:d0 + D_TILE, :, :])
+
+        def load_x(g):
+            nc.sync.dma_start(
+                out=x_raw[g][:],
+                in_=x_rows[K_PASS * g:K_PASS * (g + 1), :].rearrange("(p j) n -> p j n", j=PACK))
+
+        load_z(0)
+        load_z(1)
+        load_x(0)
+        load_x(1)
+        load_z(2)
+        load_z(3)
+
+        ident = consts.tile([P, P], F32, name="ident")
+        make_identity(nc, ident[:])
+        w_words = w_sb[:].bitcast(F32).rearrange("o (g p u) -> o g u p", g=PASSES, u=2)
+        w_ps = psum.tile([P, PASSES, 2, C_OUT], F32, name="w_ps", tag="bank")
+        for g in range(PASSES):
+            for u in range(2):
+                nc.tensor.transpose(w_ps[:, g, u, :], w_words[:, g, u, :], ident[:])
+        w_grouped = consts.tile([P, PASSES * C_OUT * PACK], BF16, name="w_grouped", align_bytes=64)
+        nc.vector.tensor_copy(
+            out=w_grouped[:].bitcast(F32).rearrange("p (g o u) -> p g o u", g=PASSES, u=2),
+            in_=w_ps[:].rearrange("p g u o -> p g o u"))
+        w_codes = consts.tile([P, PASSES * C_OUT], U32, name="w_codes", align_bytes=64)
+        w_scales = consts.tile([P, PASSES * C_OUT], U8, name="w_scales", align_bytes=64)
+
+        b_sq = consts.tile([P, P], F32, name="b_sq")
+        nc.vector.memset(b_sq[:], 0.0)
+        nc.vector.tensor_copy(out=b_sq[0:1, :], in_=b_row[:])
+        b_ps = psum.tile([P, 4 * P], F32, name="b_ps", tag="bank")
+        nc.tensor.transpose(b_ps[:, 0:P], b_sq[:], ident[:])
+        bias = consts.tile([P, 1], F32, name="bias")
+        nc.vector.tensor_copy(out=bias[:], in_=b_ps[:, 0:1])
+
+        nc.vector.quantize_mx(out=w_codes[:].bitcast(FP8X4), scales=w_scales[:], in_=w_grouped[:])
+
+        def crop_z(i):
+            zt = ostage.tile([P, D_TILE, OUT_H, OUT_W], F32, name="zt", tag="ostage")
+            nc.vector.tensor_copy(
+                out=zt[:],
+                in_=z_raw[i][:, :, MARGIN:MARGIN + OUT_H, MARGIN:MARGIN + OUT_W])
+            nc.sync.dma_start(out=out[0, C_OUT:2 * C_OUT, D_TILE * i:D_TILE * (i + 1), :, :], in_=zt[:])
+
+        crop_z(0)
+        crop_z(1)
+
+        codes = [[mx.tile([P, CHUNK], U32, name="codes%d_%d" % (g, q), align_bytes=64)
+                  for q in range(N_CHUNKS)] for g in range(PASSES)]
+        scales = [[mx.tile([P, CHUNK], U8, name="scales%d_%d" % (g, q), align_bytes=64)
+                   for q in range(N_CHUNKS)] for g in range(PASSES)]
+
+        def regroup(g, q):
+            grouped = grp.tile([P, CHUNK, PACK], BF16, name="grouped", tag="grouped", align_bytes=64)
+            nc.vector.tensor_copy(
+                out=grouped[:].rearrange("p (c i) t -> p c t i", i=4),
+                in_=x_raw[g][:, :, CHUNK * q:CHUNK * (q + 1)].rearrange("p t (c i) -> p c t i", i=4))
+            return grouped
+
+        def quantise(g, q, grouped):
+            nc.vector.quantize_mx(
+                out=codes[g][q][:].bitcast(FP8X4),
+                scales=scales[g][q][:],
+                in_=grouped[:].rearrange("p n t -> p (n t)"))
+
+        waiting = None
+        for g in range(PASSES):
+            for q in range(N_CHUNKS):
+                grouped = regroup(g, q)
+                if waiting is not None:
+                    quantise(*waiting)
+                waiting = (g, q, grouped)
+        quantise(*waiting)
+
+        def conv(m):
+            yt = ostage.tile([P, D_TILE, OUT_H, OUT_W], F32, name="yt", tag="ostage")
+            for dl in range(2):
+                cols = slice(SLICE * dl, SLICE * (dl + 1))
+                for a in range(2):
+                    rows = yt[:, 2 * dl + a, :, :].rearrange("p (hh r) (ww c) -> p r hh ww c", r=2, c=2)
+                    for r in range(2):
+                        acc = psum.tile([P, 2, SLICE], F32, name="acc", tag="bank")
+                        for c in range(2):
+                            for g in range(PASSES):
+                                o_cols = slice(C_OUT * g, C_OUT * (g + 1))
+                                nc.tensor.matmul_mx(
+                                    out=acc[:, c, :],
+                                    lhsT=w_codes[:, o_cols].bitcast(FP8X4),
+                                    lhsT_scale=w_scales[:, o_cols],
+                                    rhs=codes[g][m][:, cols].bitcast(FP8X4),
+                                    rhs_scale=scales[g][m][:, cols],
+                                    start=(g == 0),
+                                    stop=(g == PASSES - 1))
+                        nc.scalar.activation(
+                            out=rows[:, r],
+                            in_=acc[:].rearrange("p c (hh ww) -> p hh ww c", ww=W_IN),
+                            func=IDENTITY, bias=bias[:, 0:1], scale=1.0)
+            nc.sync.dma_start(out=out[0, 0:C_OUT, D_TILE * m:D_TILE * (m + 1), :, :], in_=yt[:])
+
+        conv(0)
+        conv(1)
+        crop_z(2)
+        crop_z(3)
+        conv(2)
+        conv(3)

@@ -36,7 +36,7 @@ def tile_upconvcropcat_t_kernel(tc, x, z, W, b, out):
     with tc.tile_pool(name="consts", bufs=1) as consts, \
             tc.tile_pool(name="xin", bufs=1) as xin, \
             tc.tile_pool(name="zin", bufs=1) as zin, \
-            tc.tile_pool(name="grp", bufs=4) as grp, \
+            tc.tile_pool(name="grp", bufs=3) as grp, \
             tc.tile_pool(name="mx", bufs=1) as mx, \
             tc.tile_pool(name="ostage", bufs=6) as ostage, \
             tc.psum_pool(name="psum", bufs=8) as psum:
@@ -99,9 +99,9 @@ def tile_upconvcropcat_t_kernel(tc, x, z, W, b, out):
         crop_z(0)
         crop_z(1)
 
-        codes = [[mx.tile([P, CHUNK], U32, name="codes%d_%d" % (g, q), align_bytes=64)
+        codes = [[mx.tile([P, 2, 2, SLICE], U32, name="codes%d_%d" % (g, q), align_bytes=64)
                   for q in range(N_CHUNKS)] for g in range(PASSES)]
-        scales = [[mx.tile([P, CHUNK], U8, name="scales%d_%d" % (g, q), align_bytes=64)
+        scales = [[mx.tile([P, 2, 2, SLICE], U8, name="scales%d_%d" % (g, q), align_bytes=64)
                    for q in range(N_CHUNKS)] for g in range(PASSES)]
 
         def regroup(g, q):
@@ -112,10 +112,12 @@ def tile_upconvcropcat_t_kernel(tc, x, z, W, b, out):
             return grouped
 
         def quantise(g, q, grouped):
-            nc.vector.quantize_mx(
-                out=codes[g][q][:].bitcast(FP8X4),
-                scales=scales[g][q][:],
-                in_=grouped[:].rearrange("p n t -> p (n t)"))
+            for dl in range(2):
+                for c in range(2):
+                    nc.vector.quantize_mx(
+                        out=codes[g][q][:, dl, c, :].bitcast(FP8X4),
+                        scales=scales[g][q][:, dl, c, :],
+                        in_=grouped[:, SLICE * dl:SLICE * (dl + 1), :].rearrange("p n t -> p (n t)"))
 
         waiting = None
         for g in range(PASSES):
@@ -129,22 +131,20 @@ def tile_upconvcropcat_t_kernel(tc, x, z, W, b, out):
         def conv(m):
             yt = ostage.tile([P, D_TILE, OUT_H, OUT_W], F32, name="yt", tag="ostage")
             for dl in range(2):
-                cols = slice(SLICE * dl, SLICE * (dl + 1))
                 for a in range(2):
                     rows = yt[:, 2 * dl + a, :, :].rearrange("p (hh r) (ww c) -> p r hh ww c", r=2, c=2)
                     for r in range(2):
                         acc = psum.tile([P, 2, SLICE], F32, name="acc", tag="bank")
-                        for c in range(2):
-                            for g in range(PASSES):
-                                o_cols = slice(C_OUT * g, C_OUT * (g + 1))
-                                nc.tensor.matmul_mx(
-                                    out=acc[:, c, :],
-                                    lhsT=w_codes[:, o_cols].bitcast(FP8X4),
-                                    lhsT_scale=w_scales[:, o_cols],
-                                    rhs=codes[g][m][:, cols].bitcast(FP8X4),
-                                    rhs_scale=scales[g][m][:, cols],
-                                    start=(g == 0),
-                                    stop=(g == PASSES - 1))
+                        for g in range(PASSES):
+                            o_cols = slice(C_OUT * g, C_OUT * (g + 1))
+                            nc.tensor.matmul_mx(
+                                out=acc[:].rearrange("p c n -> p (c n)"),
+                                lhsT=w_codes[:, o_cols].bitcast(FP8X4),
+                                lhsT_scale=w_scales[:, o_cols],
+                                rhs=codes[g][m][:, dl, :, :].rearrange("p c n -> p (c n)").bitcast(FP8X4),
+                                rhs_scale=scales[g][m][:, dl, :, :].rearrange("p c n -> p (c n)"),
+                                start=(g == 0),
+                                stop=(g == PASSES - 1))
                         nc.scalar.activation(
                             out=rows[:, r],
                             in_=acc[:].rearrange("p c (hh ww) -> p hh ww c", ww=W_IN),

@@ -36,7 +36,7 @@ def tile_upconvcropcat_t_kernel(tc, x, z, W, b, out):
     with tc.tile_pool(name="consts", bufs=1) as consts, \
             tc.tile_pool(name="xin", bufs=1) as xin, \
             tc.tile_pool(name="zin", bufs=1) as zin, \
-            tc.tile_pool(name="grp", bufs=3) as grp, \
+            tc.tile_pool(name="grp", bufs=4) as grp, \
             tc.tile_pool(name="mx", bufs=1) as mx, \
             tc.tile_pool(name="ostage", bufs=6) as ostage, \
             tc.psum_pool(name="psum", bufs=8) as psum:
@@ -58,12 +58,10 @@ def tile_upconvcropcat_t_kernel(tc, x, z, W, b, out):
                 out=x_raw[g][:],
                 in_=x_rows[K_PASS * g:K_PASS * (g + 1), :].rearrange("(p j) n -> p j n", j=PACK))
 
-        load_z(0)
-        load_z(1)
-        load_x(0)
-        load_x(1)
-        load_z(2)
-        load_z(3)
+        for i in range(4):
+            load_z(i)
+        for g in range(PASSES):
+            load_x(g)
 
         ident = consts.tile([P, P], F32, name="ident")
         make_identity(nc, ident[:])
@@ -96,12 +94,12 @@ def tile_upconvcropcat_t_kernel(tc, x, z, W, b, out):
                 in_=z_raw[i][:, :, MARGIN:MARGIN + OUT_H, MARGIN:MARGIN + OUT_W])
             nc.sync.dma_start(out=out[0, C_OUT:2 * C_OUT, D_TILE * i:D_TILE * (i + 1), :, :], in_=zt[:])
 
-        crop_z(0)
-        crop_z(1)
+        for i in range(4):
+            crop_z(i)
 
-        codes = [[mx.tile([P, 2, 2, SLICE], U32, name="codes%d_%d" % (g, q), align_bytes=64)
+        codes = [[mx.tile([P, CHUNK], U32, name="codes%d_%d" % (g, q), align_bytes=64)
                   for q in range(N_CHUNKS)] for g in range(PASSES)]
-        scales = [[mx.tile([P, 2, 2, SLICE], U8, name="scales%d_%d" % (g, q), align_bytes=64)
+        scales = [[mx.tile([P, CHUNK], U8, name="scales%d_%d" % (g, q), align_bytes=64)
                    for q in range(N_CHUNKS)] for g in range(PASSES)]
 
         def regroup(g, q):
@@ -112,16 +110,14 @@ def tile_upconvcropcat_t_kernel(tc, x, z, W, b, out):
             return grouped
 
         def quantise(g, q, grouped):
-            for dl in range(2):
-                for c in range(2):
-                    nc.vector.quantize_mx(
-                        out=codes[g][q][:, dl, c, :].bitcast(FP8X4),
-                        scales=scales[g][q][:, dl, c, :],
-                        in_=grouped[:, SLICE * dl:SLICE * (dl + 1), :].rearrange("p n t -> p (n t)"))
+            nc.vector.quantize_mx(
+                out=codes[g][q][:].bitcast(FP8X4),
+                scales=scales[g][q][:],
+                in_=grouped[:].rearrange("p n t -> p (n t)"))
 
         waiting = None
-        for g in range(PASSES):
-            for q in range(N_CHUNKS):
+        for q in range(N_CHUNKS):
+            for g in range(PASSES):
                 grouped = regroup(g, q)
                 if waiting is not None:
                     quantise(*waiting)
@@ -131,29 +127,27 @@ def tile_upconvcropcat_t_kernel(tc, x, z, W, b, out):
         def conv(m):
             yt = ostage.tile([P, D_TILE, OUT_H, OUT_W], F32, name="yt", tag="ostage")
             for dl in range(2):
+                cols = slice(SLICE * dl, SLICE * (dl + 1))
                 for a in range(2):
                     rows = yt[:, 2 * dl + a, :, :].rearrange("p (hh r) (ww c) -> p r hh ww c", r=2, c=2)
                     for r in range(2):
                         acc = psum.tile([P, 2, SLICE], F32, name="acc", tag="bank")
-                        for g in range(PASSES):
-                            o_cols = slice(C_OUT * g, C_OUT * (g + 1))
-                            nc.tensor.matmul_mx(
-                                out=acc[:].rearrange("p c n -> p (c n)"),
-                                lhsT=w_codes[:, o_cols].bitcast(FP8X4),
-                                lhsT_scale=w_scales[:, o_cols],
-                                rhs=codes[g][m][:, dl, :, :].rearrange("p c n -> p (c n)").bitcast(FP8X4),
-                                rhs_scale=scales[g][m][:, dl, :, :].rearrange("p c n -> p (c n)"),
-                                start=(g == 0),
-                                stop=(g == PASSES - 1))
+                        for c in range(2):
+                            for g in range(PASSES):
+                                o_cols = slice(C_OUT * g, C_OUT * (g + 1))
+                                nc.tensor.matmul_mx(
+                                    out=acc[:, c, :],
+                                    lhsT=w_codes[:, o_cols].bitcast(FP8X4),
+                                    lhsT_scale=w_scales[:, o_cols],
+                                    rhs=codes[g][m][:, cols].bitcast(FP8X4),
+                                    rhs_scale=scales[g][m][:, cols],
+                                    start=(g == 0),
+                                    stop=(g == PASSES - 1))
                         nc.scalar.activation(
                             out=rows[:, r],
                             in_=acc[:].rearrange("p c (hh ww) -> p hh ww c", ww=W_IN),
                             func=IDENTITY, bias=bias[:, 0:1], scale=1.0)
             nc.sync.dma_start(out=out[0, 0:C_OUT, D_TILE * m:D_TILE * (m + 1), :, :], in_=yt[:])
 
-        conv(0)
-        conv(1)
-        crop_z(2)
-        crop_z(3)
-        conv(2)
-        conv(3)
+        for m in range(N_CHUNKS):
+            conv(m)

@@ -36,7 +36,7 @@ def tile_upconvcropcat_t_kernel(tc, x, z, W, b, out):
     with tc.tile_pool(name="consts", bufs=1) as consts, \
             tc.tile_pool(name="xin", bufs=1) as xin, \
             tc.tile_pool(name="zin", bufs=1) as zin, \
-            tc.tile_pool(name="grp", bufs=4) as grp, \
+            tc.tile_pool(name="grp", bufs=3) as grp, \
             tc.tile_pool(name="mx", bufs=1) as mx, \
             tc.tile_pool(name="ostage", bufs=6) as ostage, \
             tc.psum_pool(name="psum", bufs=8) as psum:
@@ -97,9 +97,9 @@ def tile_upconvcropcat_t_kernel(tc, x, z, W, b, out):
         for i in range(4):
             crop_z(i)
 
-        codes = [[mx.tile([P, CHUNK], U32, name="codes%d_%d" % (g, q), align_bytes=64)
+        codes = [[mx.tile([P, 2, 2, SLICE], U32, name="codes%d_%d" % (g, q), align_bytes=64)
                   for q in range(N_CHUNKS)] for g in range(PASSES)]
-        scales = [[mx.tile([P, CHUNK], U8, name="scales%d_%d" % (g, q), align_bytes=64)
+        scales = [[mx.tile([P, 2, 2, SLICE], U8, name="scales%d_%d" % (g, q), align_bytes=64)
                    for q in range(N_CHUNKS)] for g in range(PASSES)]
 
         def regroup(g, q):
@@ -110,10 +110,12 @@ def tile_upconvcropcat_t_kernel(tc, x, z, W, b, out):
             return grouped
 
         def quantise(g, q, grouped):
-            nc.vector.quantize_mx(
-                out=codes[g][q][:].bitcast(FP8X4),
-                scales=scales[g][q][:],
-                in_=grouped[:].rearrange("p n t -> p (n t)"))
+            for dl in range(2):
+                for c in range(2):
+                    nc.vector.quantize_mx(
+                        out=codes[g][q][:, dl, c, :].bitcast(FP8X4),
+                        scales=scales[g][q][:, dl, c, :],
+                        in_=grouped[:, SLICE * dl:SLICE * (dl + 1), :].rearrange("p n t -> p (n t)"))
 
         waiting = None
         for q in range(N_CHUNKS):
@@ -127,22 +129,20 @@ def tile_upconvcropcat_t_kernel(tc, x, z, W, b, out):
         def conv(m):
             yt = ostage.tile([P, D_TILE, OUT_H, OUT_W], F32, name="yt", tag="ostage")
             for dl in range(2):
-                cols = slice(SLICE * dl, SLICE * (dl + 1))
                 for a in range(2):
                     rows = yt[:, 2 * dl + a, :, :].rearrange("p (hh r) (ww c) -> p r hh ww c", r=2, c=2)
                     for r in range(2):
                         acc = psum.tile([P, 2, SLICE], F32, name="acc", tag="bank")
-                        for c in range(2):
-                            for g in range(PASSES):
-                                o_cols = slice(C_OUT * g, C_OUT * (g + 1))
-                                nc.tensor.matmul_mx(
-                                    out=acc[:, c, :],
-                                    lhsT=w_codes[:, o_cols].bitcast(FP8X4),
-                                    lhsT_scale=w_scales[:, o_cols],
-                                    rhs=codes[g][m][:, cols].bitcast(FP8X4),
-                                    rhs_scale=scales[g][m][:, cols],
-                                    start=(g == 0),
-                                    stop=(g == PASSES - 1))
+                        for g in range(PASSES):
+                            o_cols = slice(C_OUT * g, C_OUT * (g + 1))
+                            nc.tensor.matmul_mx(
+                                out=acc[:].rearrange("p c n -> p (c n)"),
+                                lhsT=w_codes[:, o_cols].bitcast(FP8X4),
+                                lhsT_scale=w_scales[:, o_cols],
+                                rhs=codes[g][m][:, dl, :, :].rearrange("p c n -> p (c n)").bitcast(FP8X4),
+                                rhs_scale=scales[g][m][:, dl, :, :].rearrange("p c n -> p (c n)"),
+                                start=(g == 0),
+                                stop=(g == PASSES - 1))
                         nc.scalar.activation(
                             out=rows[:, r],
                             in_=acc[:].rearrange("p c (hh ww) -> p hh ww c", ww=W_IN),

@@ -7,22 +7,29 @@ U32 = mybir.dt.uint32
 U8 = mybir.dt.uint8
 FP8X4 = mybir.dt.float8_e4m3fn_x4
 IDENTITY = mybir.ActivationFunctionType.Identity
+ADD = mybir.AluOpType.add
 
 P = 128
 PACK = 4
 K_PASS = P * PACK
+HALVES = 2
+RUN = 4
+UP = 2
 C_IN = 1024
 PASSES = C_IN // K_PASS
 C_OUT = 128
 D_IN, H_IN, W_IN = 8, 16, 16
 POS = D_IN * H_IN * W_IN
 SLICE = H_IN * W_IN
-CHUNK = 2 * SLICE
+SLICES = 2
+CHUNK = SLICES * SLICE
 N_CHUNKS = POS // CHUNK
 Z_SIDE = 36
 MARGIN = 2
 OUT_D, OUT_H, OUT_W = 16, 32, 32
-D_TILE = 4
+D_TILE = UP * SLICES
+N_TILES = OUT_D // D_TILE
+BANK = 512
 
 FLOPS = 2 * C_OUT * C_IN * OUT_D * OUT_H * OUT_W
 BYTES = (C_IN * POS * 2 + C_OUT * OUT_D * OUT_H * OUT_W * 2 + C_OUT * C_IN * 2 + C_OUT * 2
@@ -36,7 +43,7 @@ def tile_upconvcropcat_t_kernel(tc, x, z, W, b, out):
     with tc.tile_pool(name="consts", bufs=1) as consts, \
             tc.tile_pool(name="xin", bufs=1) as xin, \
             tc.tile_pool(name="zin", bufs=1) as zin, \
-            tc.tile_pool(name="grp", bufs=3) as grp, \
+            tc.tile_pool(name="grp", bufs=4) as grp, \
             tc.tile_pool(name="mx", bufs=1) as mx, \
             tc.tile_pool(name="ostage", bufs=6) as ostage, \
             tc.psum_pool(name="psum", bufs=8) as psum:
@@ -46,76 +53,93 @@ def tile_upconvcropcat_t_kernel(tc, x, z, W, b, out):
         b_row = consts.tile([1, C_OUT], BF16, name="b_row")
         nc.scalar.dma_start(out=b_row[:], in_=b.unsqueeze(0))
 
-        z_raw = [zin.tile([P, D_TILE, Z_SIDE, Z_SIDE], BF16, name="z_raw%d" % i) for i in range(4)]
+        z_raw = [zin.tile([P, D_TILE, Z_SIDE, Z_SIDE], BF16, name="z_raw%d" % part) for part in range(N_TILES)]
         x_raw = [xin.tile([P, PACK, POS], BF16, name="x_raw%d" % g) for g in range(PASSES)]
 
-        def load_z(i):
-            d0 = MARGIN + D_TILE * i
-            nc.sync.dma_start(out=z_raw[i][:], in_=z[0, :, d0:d0 + D_TILE, :, :])
-
-        def load_x(g):
+        for part in range(N_TILES):
+            first = MARGIN + D_TILE * part
+            nc.sync.dma_start(out=z_raw[part][:], in_=z[0, :, first:first + D_TILE, :, :])
+        for g in range(PASSES):
             nc.sync.dma_start(
                 out=x_raw[g][:],
-                in_=x_rows[K_PASS * g:K_PASS * (g + 1), :].rearrange("(p j) n -> p j n", j=PACK))
-
-        for i in range(4):
-            load_z(i)
-        for g in range(PASSES):
-            load_x(g)
+                in_=x_rows[K_PASS * g:K_PASS * (g + 1), :].rearrange("(p t) n -> p t n", t=PACK))
 
         ident = consts.tile([P, P], F32, name="ident")
         make_identity(nc, ident[:])
-        w_words = w_sb[:].bitcast(F32).rearrange("o (g p u) -> o g u p", g=PASSES, u=2)
-        w_ps = psum.tile([P, PASSES, 2, C_OUT], F32, name="w_ps", tag="bank")
+        w_words = w_sb[:].bitcast(F32).rearrange("o (g p v) -> o g v p", g=PASSES, v=HALVES)
+        w_ps = psum.tile([P, PASSES, HALVES, C_OUT], F32, name="w_ps", tag="bank")
         for g in range(PASSES):
-            for u in range(2):
-                nc.tensor.transpose(w_ps[:, g, u, :], w_words[:, g, u, :], ident[:])
+            for v in range(HALVES):
+                nc.tensor.transpose(w_ps[:, g, v, :], w_words[:, g, v, :], ident[:])
         w_grouped = consts.tile([P, PASSES * C_OUT * PACK], BF16, name="w_grouped", align_bytes=64)
         nc.vector.tensor_copy(
-            out=w_grouped[:].bitcast(F32).rearrange("p (g o u) -> p g o u", g=PASSES, u=2),
-            in_=w_ps[:].rearrange("p g u o -> p g o u"))
+            out=w_grouped[:].bitcast(F32).rearrange("p (g o v) -> p g o v", g=PASSES, v=HALVES),
+            in_=w_ps[:].rearrange("p g v o -> p g o v"))
         w_codes = consts.tile([P, PASSES * C_OUT], U32, name="w_codes", align_bytes=64)
         w_scales = consts.tile([P, PASSES * C_OUT], U8, name="w_scales", align_bytes=64)
 
         b_sq = consts.tile([P, P], F32, name="b_sq")
         nc.vector.memset(b_sq[:], 0.0)
         nc.vector.tensor_copy(out=b_sq[0:1, :], in_=b_row[:])
-        b_ps = psum.tile([P, 4 * P], F32, name="b_ps", tag="bank")
+        b_ps = psum.tile([P, BANK], F32, name="b_ps", tag="bank")
         nc.tensor.transpose(b_ps[:, 0:P], b_sq[:], ident[:])
         bias = consts.tile([P, 1], F32, name="bias")
         nc.vector.tensor_copy(out=bias[:], in_=b_ps[:, 0:1])
 
         nc.vector.quantize_mx(out=w_codes[:].bitcast(FP8X4), scales=w_scales[:], in_=w_grouped[:])
 
-        def crop_z(i):
+        for part in range(N_TILES):
             zt = ostage.tile([P, D_TILE, OUT_H, OUT_W], F32, name="zt", tag="ostage")
             nc.vector.tensor_copy(
                 out=zt[:],
-                in_=z_raw[i][:, :, MARGIN:MARGIN + OUT_H, MARGIN:MARGIN + OUT_W])
-            nc.sync.dma_start(out=out[0, C_OUT:2 * C_OUT, D_TILE * i:D_TILE * (i + 1), :, :], in_=zt[:])
+                in_=z_raw[part][:, :, MARGIN:MARGIN + OUT_H, MARGIN:MARGIN + OUT_W])
+            nc.sync.dma_start(out=out[0, C_OUT:2 * C_OUT, D_TILE * part:D_TILE * (part + 1), :, :], in_=zt[:])
 
-        for i in range(4):
-            crop_z(i)
-
-        codes = [[mx.tile([P, 2, 2, SLICE], U32, name="codes%d_%d" % (g, q), align_bytes=64)
+        codes = [[mx.tile([P, CHUNK], U32, name="codes%d_%d" % (g, q), align_bytes=64)
                   for q in range(N_CHUNKS)] for g in range(PASSES)]
-        scales = [[mx.tile([P, 2, 2, SLICE], U8, name="scales%d_%d" % (g, q), align_bytes=64)
+        scales = [[mx.tile([P, CHUNK], U8, name="scales%d_%d" % (g, q), align_bytes=64)
                    for q in range(N_CHUNKS)] for g in range(PASSES)]
 
         def regroup(g, q):
             grouped = grp.tile([P, CHUNK, PACK], BF16, name="grouped", tag="grouped", align_bytes=64)
             nc.vector.tensor_copy(
-                out=grouped[:].rearrange("p (c i) t -> p c t i", i=4),
-                in_=x_raw[g][:, :, CHUNK * q:CHUNK * (q + 1)].rearrange("p t (c i) -> p c t i", i=4))
+                out=grouped[:].rearrange("p (run e) t -> p run t e", e=RUN),
+                in_=x_raw[g][:, :, CHUNK * q:CHUNK * (q + 1)].rearrange("p t (run e) -> p run t e", e=RUN))
             return grouped
 
         def quantise(g, q, grouped):
-            for dl in range(2):
-                for c in range(2):
-                    nc.vector.quantize_mx(
-                        out=codes[g][q][:, dl, c, :].bitcast(FP8X4),
-                        scales=scales[g][q][:, dl, c, :],
-                        in_=grouped[:, SLICE * dl:SLICE * (dl + 1), :].rearrange("p n t -> p (n t)"))
+            nc.vector.quantize_mx(
+                out=codes[g][q][:].bitcast(FP8X4),
+                scales=scales[g][q][:],
+                in_=grouped[:].rearrange("p n t -> p (n t)"))
+
+        def convolve(q):
+            yt = ostage.tile([P, D_TILE, OUT_H, OUT_W], F32, name="yt", tag="ostage")
+            for d in range(SLICES):
+                cols = slice(SLICE * d, SLICE * (d + 1))
+                for od in range(UP):
+                    rows = yt[:, UP * d + od, :, :].rearrange("p (h oh) (w ow) -> p oh h w ow", oh=UP, ow=UP)
+                    for oh in range(UP):
+                        acc = psum.tile([P, UP, SLICE], F32, name="acc", tag="bank")
+                        for ow in range(UP):
+                            for g in range(PASSES):
+                                o_cols = slice(C_OUT * g, C_OUT * (g + 1))
+                                nc.tensor.matmul_mx(
+                                    out=acc[:, ow, :],
+                                    lhsT=w_codes[:, o_cols].bitcast(FP8X4),
+                                    lhsT_scale=w_scales[:, o_cols],
+                                    rhs=codes[g][q][:, cols].bitcast(FP8X4),
+                                    rhs_scale=scales[g][q][:, cols],
+                                    start=(g == 0),
+                                    stop=(g == PASSES - 1))
+                        sums = acc[:].rearrange("p ow (h w) -> p h w ow", w=W_IN)
+                        if od == UP - 1 and oh == UP - 1:
+                            nc.vector.tensor_scalar(
+                                out=rows[:, oh], in0=sums, scalar1=bias[:, 0:1], scalar2=None, op0=ADD)
+                        else:
+                            nc.scalar.activation(
+                                out=rows[:, oh], in_=sums, func=IDENTITY, bias=bias[:, 0:1], scale=1.0)
+            nc.sync.dma_start(out=out[0, 0:C_OUT, D_TILE * q:D_TILE * (q + 1), :, :], in_=yt[:])
 
         waiting = None
         for q in range(N_CHUNKS):
@@ -124,30 +148,7 @@ def tile_upconvcropcat_t_kernel(tc, x, z, W, b, out):
                 if waiting is not None:
                     quantise(*waiting)
                 waiting = (g, q, grouped)
+            if q > 0:
+                convolve(q - 1)
         quantise(*waiting)
-
-        def conv(m):
-            yt = ostage.tile([P, D_TILE, OUT_H, OUT_W], F32, name="yt", tag="ostage")
-            for dl in range(2):
-                for a in range(2):
-                    rows = yt[:, 2 * dl + a, :, :].rearrange("p (hh r) (ww c) -> p r hh ww c", r=2, c=2)
-                    for r in range(2):
-                        acc = psum.tile([P, 2, SLICE], F32, name="acc", tag="bank")
-                        for g in range(PASSES):
-                            o_cols = slice(C_OUT * g, C_OUT * (g + 1))
-                            nc.tensor.matmul_mx(
-                                out=acc[:].rearrange("p c n -> p (c n)"),
-                                lhsT=w_codes[:, o_cols].bitcast(FP8X4),
-                                lhsT_scale=w_scales[:, o_cols],
-                                rhs=codes[g][m][:, dl, :, :].rearrange("p c n -> p (c n)").bitcast(FP8X4),
-                                rhs_scale=scales[g][m][:, dl, :, :].rearrange("p c n -> p (c n)"),
-                                start=(g == 0),
-                                stop=(g == PASSES - 1))
-                        nc.scalar.activation(
-                            out=rows[:, r],
-                            in_=acc[:].rearrange("p c (hh ww) -> p hh ww c", ww=W_IN),
-                            func=IDENTITY, bias=bias[:, 0:1], scale=1.0)
-            nc.sync.dma_start(out=out[0, 0:C_OUT, D_TILE * m:D_TILE * (m + 1), :, :], in_=yt[:])
-
-        for m in range(N_CHUNKS):
-            conv(m)
+        convolve(N_CHUNKS - 1)

import concourse.mybir as mybir
from concourse.masks import make_identity

F32 = mybir.dt.float32
BF16 = mybir.dt.bfloat16
U32 = mybir.dt.uint32
U8 = mybir.dt.uint8
FP8X4 = mybir.dt.float8_e4m3fn_x4
IDENTITY = mybir.ActivationFunctionType.Identity
ADD = mybir.AluOpType.add

P = 128
PACK = 4
K_PASS = P * PACK
HALVES = 2
RUN = 4
UP = 2
C_IN = 1024
PASSES = C_IN // K_PASS
C_OUT = 128
D_IN, H_IN, W_IN = 8, 16, 16
POS = D_IN * H_IN * W_IN
SLICE = H_IN * W_IN
SLICES = 2
CHUNK = SLICES * SLICE
N_CHUNKS = POS // CHUNK
Z_SIDE = 36
MARGIN = 2
OUT_D, OUT_H, OUT_W = 16, 32, 32
D_TILE = UP * SLICES
N_TILES = OUT_D // D_TILE
BANK = 512

FLOPS = 2 * C_OUT * C_IN * OUT_D * OUT_H * OUT_W
BYTES = (C_IN * POS * 2 + C_OUT * OUT_D * OUT_H * OUT_W * 2 + C_OUT * C_IN * 2 + C_OUT * 2
         + 2 * C_OUT * OUT_D * OUT_H * OUT_W * 4)


def tile_upconvcropcat_t_kernel(tc, x, z, W, b, out):
    nc = tc.nc
    x_rows = x[0].rearrange("c d h w -> c (d h w)")

    with tc.tile_pool(name="consts", bufs=1) as consts, \
            tc.tile_pool(name="xin", bufs=1) as xin, \
            tc.tile_pool(name="zin", bufs=1) as zin, \
            tc.tile_pool(name="grp", bufs=4) as grp, \
            tc.tile_pool(name="mx", bufs=1) as mx, \
            tc.tile_pool(name="ostage", bufs=6) as ostage, \
            tc.psum_pool(name="psum", bufs=8) as psum:

        w_sb = consts.tile([P, C_IN], BF16, name="w_sb")
        nc.scalar.dma_start(out=w_sb[:], in_=W)
        b_row = consts.tile([1, C_OUT], BF16, name="b_row")
        nc.scalar.dma_start(out=b_row[:], in_=b.unsqueeze(0))

        z_raw = [zin.tile([P, D_TILE, Z_SIDE, Z_SIDE], BF16, name="z_raw%d" % part) for part in range(N_TILES)]
        x_raw = [xin.tile([P, PACK, POS], BF16, name="x_raw%d" % g) for g in range(PASSES)]

        for part in range(N_TILES):
            first = MARGIN + D_TILE * part
            nc.sync.dma_start(out=z_raw[part][:], in_=z[0, :, first:first + D_TILE, :, :])
        for g in range(PASSES):
            nc.sync.dma_start(
                out=x_raw[g][:],
                in_=x_rows[K_PASS * g:K_PASS * (g + 1), :].rearrange("(p t) n -> p t n", t=PACK))

        ident = consts.tile([P, P], F32, name="ident")
        make_identity(nc, ident[:])
        w_words = w_sb[:].bitcast(F32).rearrange("o (g p v) -> o g v p", g=PASSES, v=HALVES)
        w_ps = psum.tile([P, PASSES, HALVES, C_OUT], F32, name="w_ps", tag="bank")
        for g in range(PASSES):
            for v in range(HALVES):
                nc.tensor.transpose(w_ps[:, g, v, :], w_words[:, g, v, :], ident[:])
        w_grouped = consts.tile([P, PASSES * C_OUT * PACK], BF16, name="w_grouped", align_bytes=64)
        nc.vector.tensor_copy(
            out=w_grouped[:].bitcast(F32).rearrange("p (g o v) -> p g o v", g=PASSES, v=HALVES),
            in_=w_ps[:].rearrange("p g v o -> p g o v"))
        w_codes = consts.tile([P, PASSES * C_OUT], U32, name="w_codes", align_bytes=64)
        w_scales = consts.tile([P, PASSES * C_OUT], U8, name="w_scales", align_bytes=64)

        b_sq = consts.tile([P, P], F32, name="b_sq")
        nc.vector.memset(b_sq[:], 0.0)
        nc.vector.tensor_copy(out=b_sq[0:1, :], in_=b_row[:])
        b_ps = psum.tile([P, BANK], F32, name="b_ps", tag="bank")
        nc.tensor.transpose(b_ps[:, 0:P], b_sq[:], ident[:])
        bias = consts.tile([P, 1], F32, name="bias")
        nc.vector.tensor_copy(out=bias[:], in_=b_ps[:, 0:1])

        nc.vector.quantize_mx(out=w_codes[:].bitcast(FP8X4), scales=w_scales[:], in_=w_grouped[:])

        for part in range(N_TILES):
            zt = ostage.tile([P, D_TILE, OUT_H, OUT_W], F32, name="zt", tag="ostage")
            nc.vector.tensor_copy(
                out=zt[:],
                in_=z_raw[part][:, :, MARGIN:MARGIN + OUT_H, MARGIN:MARGIN + OUT_W])
            nc.sync.dma_start(out=out[0, C_OUT:2 * C_OUT, D_TILE * part:D_TILE * (part + 1), :, :], in_=zt[:])

        codes = [[mx.tile([P, CHUNK], U32, name="codes%d_%d" % (g, q), align_bytes=64)
                  for q in range(N_CHUNKS)] for g in range(PASSES)]
        scales = [[mx.tile([P, CHUNK], U8, name="scales%d_%d" % (g, q), align_bytes=64)
                   for q in range(N_CHUNKS)] for g in range(PASSES)]

        def regroup(g, q):
            grouped = grp.tile([P, CHUNK, PACK], BF16, name="grouped", tag="grouped", align_bytes=64)
            nc.vector.tensor_copy(
                out=grouped[:].rearrange("p (run e) t -> p run t e", e=RUN),
                in_=x_raw[g][:, :, CHUNK * q:CHUNK * (q + 1)].rearrange("p t (run e) -> p run t e", e=RUN))
            return grouped

        def quantise(g, q, grouped):
            nc.vector.quantize_mx(
                out=codes[g][q][:].bitcast(FP8X4),
                scales=scales[g][q][:],
                in_=grouped[:].rearrange("p n t -> p (n t)"))

        def convolve(q):
            yt = ostage.tile([P, D_TILE, OUT_H, OUT_W], F32, name="yt", tag="ostage")
            for d in range(SLICES):
                cols = slice(SLICE * d, SLICE * (d + 1))
                for od in range(UP):
                    rows = yt[:, UP * d + od, :, :].rearrange("p (h oh) (w ow) -> p oh h w ow", oh=UP, ow=UP)
                    for oh in range(UP):
                        acc = psum.tile([P, UP, SLICE], F32, name="acc", tag="bank")
                        for ow in range(UP):
                            for g in range(PASSES):
                                o_cols = slice(C_OUT * g, C_OUT * (g + 1))
                                nc.tensor.matmul_mx(
                                    out=acc[:, ow, :],
                                    lhsT=w_codes[:, o_cols].bitcast(FP8X4),
                                    lhsT_scale=w_scales[:, o_cols],
                                    rhs=codes[g][q][:, cols].bitcast(FP8X4),
                                    rhs_scale=scales[g][q][:, cols],
                                    start=(g == 0),
                                    stop=(g == PASSES - 1))
                        sums = acc[:].rearrange("p ow (h w) -> p h w ow", w=W_IN)
                        if od == UP - 1 and oh == UP - 1:
                            nc.vector.tensor_scalar(
                                out=rows[:, oh], in0=sums, scalar1=bias[:, 0:1], scalar2=None, op0=ADD)
                        else:
                            nc.scalar.activation(
                                out=rows[:, oh], in_=sums, func=IDENTITY, bias=bias[:, 0:1], scale=1.0)
            nc.sync.dma_start(out=out[0, 0:C_OUT, D_TILE * q:D_TILE * (q + 1), :, :], in_=yt[:])

        waiting = None
        for q in range(N_CHUNKS):
            for g in range(PASSES):
                grouped = regroup(g, q)
                if waiting is not None:
                    quantise(*waiting)
                waiting = (g, q, grouped)
            if q > 0:
                convolve(q - 1)
        quantise(*waiting)
        convolve(N_CHUNKS - 1)
